import numpy as np
import ml_dtypes


def mxq(x, axis, fmt="e4m3"):
    dtype, down = {"e4m3": (ml_dtypes.float8_e4m3fn, 7), "e5m2": (ml_dtypes.float8_e5m2, 14)}[fmt]
    v = np.moveaxis(np.asarray(x, np.float32).astype(ml_dtypes.bfloat16).astype(np.float64), axis, -1)
    blocks = v.reshape(v.shape[:-1] + (-1, 32))
    amax = np.abs(blocks).max(-1, keepdims=True)
    byte = np.maximum(np.where(amax > 0, np.frexp(amax)[1] - 1 + 127, 0) - down, 1)
    scale = np.exp2(byte - 127.0)
    codes = (blocks / scale).astype(np.float32).astype(dtype).astype(np.float64)
    return np.moveaxis((codes * scale).reshape(v.shape), -1, axis)


WIDE = False


def mx_kscale(k):
    if not WIDE:
        return np.ones(k)
    levels = np.array([20, -20, 10, -10, 0])
    a = np.random.permutation(np.resize(levels, k // 512 * 4)).reshape(k // 512, 4)
    idx = np.arange(k)
    return np.exp2(a[idx // 512, idx % 128 // 32])


BF16 = ml_dtypes.bfloat16


def bf(x):
    return np.asarray(x, np.float32).astype(BF16)


def f64(x):
    return np.asarray(x).astype(np.float64)


B, T, C, R, H, DN, DR, DV = 2, 256, 512, 512, 16, 960, 64, 128
DQ = DN + DR
NF = DR // 2


def rotate_half(u):
    u1, u2 = u[..., : u.shape[-1] // 2], u[..., u.shape[-1] // 2 :]
    return np.concatenate([-u2, u1], axis=-1)


def setup_inputs():
    u = np.array(mx_kscale(H * DQ), dtype=np.float64).reshape(H, DQ)
    u[:, DN + NF :] = u[:, DN : DN + NF]
    x = np.random.standard_normal((B, T, C))
    freqs_cis = np.stack([np.random.uniform(size=(T, NF)), np.random.uniform(size=(T, NF))], axis=-1)
    w_q = np.random.standard_normal((C, H * DQ)) / np.sqrt(C) / u.reshape(1, H * DQ)
    g = np.random.standard_normal((B, T, H, DQ)) * np.exp2(np.random.randint(-12, 1, (B, T, 1, 1))) * 4.0 * u
    return {"x": bf(x), "freqs_cis": bf(freqs_cis), "w_q": bf(w_q), "grad_out": bf(g)}


def reference(x, freqs_cis, w_q, grad_out):
    g = f64(grad_out)
    freqs = f64(freqs_cis)
    cos = freqs[..., 0][None, :, None, :]
    sin = freqs[..., 1][None, :, None, :]
    g1 = g[..., DN : DN + NF]
    g2 = g[..., DN + NF :]
    gq = np.concatenate([g[..., :DN], g1 * cos + g2 * sin, g2 * cos - g1 * sin], axis=-1).reshape(B, T, H * DQ)
    return mxq(gq, 2, "e5m2") @ mxq(f64(w_q), 1, "e4m3").T

@@ -1,0 +1,206 @@
+from contextlib import ExitStack
+
+import concourse.mybir as mybir
+from concourse.masks import make_identity
+
+F32 = mybir.dt.float32
+BF16 = mybir.dt.bfloat16
+U32 = mybir.dt.uint32
+U8 = mybir.dt.uint8
+E5M2_X4 = mybir.dt.float8_e5m2_x4
+E4M3_X4 = mybir.dt.float8_e4m3fn_x4
+MULT = mybir.AluOpType.mult
+ADD = mybir.AluOpType.add
+
+P = 128
+B, T, C, H = 2, 256, 512, 16
+DN, DR = 960, 64
+DQ = DN + DR
+NF = DR // 2
+TOKENS = B * T
+ROW_TILES = TOKENS // P
+T_TILES = T // P
+
+WINDOW = 256
+K_PASS = 2 * WINDOW
+PASSES = H * DQ // K_PASS
+PASSES_PER_HEAD = DQ // K_PASS
+BLOCK = 32
+RUN = BLOCK // 2
+ROT_IN_WINDOW = DN % WINDOW
+
+RAW_BUFS = 8
+MX_LAG = 2
+
+FLOPS = 2 * TOKENS * C * H * DQ
+BYTES = 2 * (TOKENS + C) * H * DQ + 2 * T * DR + 4 * TOKENS * C
+
+
+def runs_that_change_places(head_tile):
+    words = head_tile[:].bitcast(F32)
+    plain = words[:, :, (DN - WINDOW) // 2 : (DN - WINDOW + DR) // 2]
+    rotated = words[:, :, DN // 2 : DQ // 2]
+    plain_second = plain.rearrange("p a (i c) -> p a i c", c=BLOCK // 2)[:, :, :, RUN // 2 :]
+    rotated_first = rotated.rearrange("p a (i c) -> p a i c", c=BLOCK // 2)[:, :, :, : RUN // 2]
+    return plain_second, rotated_first
+
+
+def tile_fa3mlaattention_pb_k_kernel(tc, x, freqs_cis, w_q, grad_out, out):
+    nc = tc.nc
+    g_heads = grad_out.rearrange("b (t p) h c -> p (b t) h c", p=P)
+    w_heads = w_q.rearrange("(a p) (h c) -> p a h c", p=P, c=DQ)
+    out_tiles = out.rearrange("b (t p) c -> (b t) p c", p=P)
+
+    with ExitStack() as ctx:
+        consts = ctx.enter_context(tc.tile_pool(name="consts", bufs=1))
+        raw = ctx.enter_context(tc.tile_pool(name="raw", bufs=RAW_BUFS))
+        rot = ctx.enter_context(tc.tile_pool(name="rot", bufs=2))
+        mx = ctx.enter_context(tc.tile_pool(name="mx", bufs=MX_LAG + 1))
+        results = ctx.enter_context(tc.tile_pool(name="results", bufs=1))
+        sums = ctx.enter_context(tc.psum_pool(name="sums", bufs=1))
+        flipped = ctx.enter_context(tc.psum_pool(name="flipped", bufs=1))
+        ctx.enter_context(tc.manual_schedule())
+
+        g_raw = {}
+        w_raw = {}
+
+        def load_head(h):
+            g_raw[h] = raw.tile([P, ROW_TILES, DQ], BF16, name="g_raw", tag="g_raw")
+            nc.sync.dma_start(out=g_raw[h][:], in_=g_heads[:, :, h, :])
+            w_raw[h] = raw.tile([P, ROW_TILES, DQ], BF16, name="w_raw", tag="w_raw")
+            nc.sync.dma_start(out=w_raw[h][:], in_=w_heads[:, :, h, :])
+
+        freqs = consts.tile([P, T_TILES, NF, 2], BF16)
+        nc.scalar.dma_start(out=freqs[:], in_=freqs_cis.rearrange("(t p) j c -> p t j c", p=P))
+        for h in range(RAW_BUFS - 1):
+            load_head(h)
+
+        ident = consts.tile([P, P], F32)
+        make_identity(nc, ident[:])
+
+        cos_cos = consts.tile([P, T_TILES, 2, NF], BF16)
+        nc.vector.tensor_copy(
+            out=cos_cos[:], in_=freqs[:, :, :, 0].unsqueeze(2).to_broadcast([P, T_TILES, 2, NF])
+        )
+        sin_sin = consts.tile([P, T_TILES, 2, NF], BF16)
+        nc.vector.tensor_scalar(
+            out=sin_sin[:, :, 0, :], in0=freqs[:, :, :, 1], scalar1=-1.0, scalar2=None, op0=MULT
+        )
+        nc.vector.tensor_copy(out=sin_sin[:, :, 1, :], in_=freqs[:, :, :, 1])
+
+        def for_both_batches(table):
+            return (
+                table[:]
+                .rearrange("p t f j -> p t (f j)")
+                .unsqueeze(1)
+                .to_broadcast([P, B, T_TILES, DR])
+            )
+
+        def prepare_head(h):
+            g_tile = g_raw[h]
+            g_rot = g_tile[:].rearrange("p (b t) c -> p b t c", b=B)[:, :, :, DN:DQ]
+            by_cos = rot.tile([P, B, T_TILES, DR], F32)
+            nc.vector.tensor_tensor(out=by_cos[:], in0=g_rot, in1=for_both_batches(cos_cos), op=MULT)
+            by_sin = rot.tile([P, B, T_TILES, DR], F32)
+            nc.vector.tensor_tensor(out=by_sin[:], in0=g_rot, in1=for_both_batches(sin_sin), op=MULT)
+
+            plain_second, rotated_first = runs_that_change_places(g_tile)
+            nc.vector.tensor_copy(out=rotated_first, in_=plain_second)
+
+            split = "p b t (f r m) -> p (b t) f r m"
+            cos_runs = by_cos[:].rearrange(split, f=2, r=2)
+            sin_runs = by_sin[:].rearrange(split, f=2, r=2)
+            windows = g_tile[:, :, K_PASS:DQ].rearrange("p a (r c) -> p a r c", r=2)
+            for f in range(2):
+                lo = ROT_IN_WINDOW + BLOCK * f + RUN
+                nc.vector.tensor_tensor(
+                    out=windows[:, :, :, lo : lo + RUN],
+                    in0=cos_runs[:, :, f],
+                    in1=sin_runs[:, :, 1 - f],
+                    op=ADD,
+                )
+
+            plain_second, rotated_first = runs_that_change_places(w_raw[h])
+            parked = rot.tile([P, ROW_TILES, DR // BLOCK, RUN // 2], F32)
+            nc.scalar.copy(out=parked[:], in_=plain_second)
+            nc.scalar.copy(out=plain_second, in_=rotated_first)
+            nc.scalar.copy(out=rotated_first, in_=parked[:])
+
+        grouped = {}
+        codes = {}
+        scales = {}
+
+        def transpose_pass(s):
+            h = s // PASSES_PER_HEAD
+            first_word = (s % PASSES_PER_HEAD) * K_PASS // 2
+            for name, head_tile in (("g", g_raw[h]), ("w", w_raw[h])):
+                words = head_tile[:].bitcast(F32)
+                grouped[name, s] = mx.tile(
+                    [P, 4 * TOKENS], BF16, name=name + "_grouped", tag=name + "_grouped", align_bytes=64
+                )
+                pairs = grouped[name, s][:].bitcast(F32).rearrange("p (n u) -> p n u", u=2)
+                for half in range(ROW_TILES // 2):
+                    bank_name = "%s_bank%d" % (name, half)
+                    bank = flipped.tile([P, 2, 2 * P], F32, name=bank_name, tag=bank_name)
+                    for i in range(2):
+                        for u in range(2):
+                            lo = first_word + u * P
+                            nc.tensor.transpose(
+                                bank[:, u, i * P : (i + 1) * P],
+                                words[:, 2 * half + i, lo : lo + P],
+                                ident[:],
+                            )
+                    last_bank = name == "w" and half == ROW_TILES // 2 - 1
+                    copy = nc.vector.tensor_copy if last_bank and s % PASSES_PER_HEAD == 0 else nc.scalar.copy
+                    copy(
+                        out=pairs[:, 2 * half * P : 2 * (half + 1) * P, :],
+                        in_=bank[:].rearrange("p u n -> p n u"),
+                    )
+
+        def quantise_pass(s):
+            for name, fp8 in (("g", E5M2_X4), ("w", E4M3_X4)):
+                codes[name, s] = mx.tile(
+                    [P, TOKENS], U32, name=name + "_codes", tag=name + "_codes", align_bytes=64
+                )
+                scales[name, s] = mx.tile(
+                    [P, TOKENS], U8, name=name + "_scales", tag=name + "_scales", align_bytes=64
+                )
+                nc.vector.quantize_mx(
+                    out=codes[name, s][:].bitcast(fp8), scales=scales[name, s][:], in_=grouped[name, s][:]
+                )
+
+        acc = [sums.tile([P, C], F32, name="acc%d" % a, tag="acc%d" % a) for a in range(ROW_TILES)]
+
+        def multiply_pass(s):
+            for a in range(ROW_TILES):
+                tokens = slice(a * P, (a + 1) * P)
+                nc.tensor.matmul_mx(
+                    out=acc[a][:],
+                    lhsT=codes["g", s][:, tokens].bitcast(E5M2_X4),
+                    lhsT_scale=scales["g", s][:, tokens],
+                    rhs=codes["w", s][:].bitcast(E4M3_X4),
+                    rhs_scale=scales["w", s][:],
+                    start=(s == 0),
+                    stop=(s == PASSES - 1),
+                )
+
+        prepare_head(0)
+        for step in range(PASSES + MX_LAG):
+            h = step // PASSES_PER_HEAD
+            first_of_head = step % PASSES_PER_HEAD == 0
+            if first_of_head and h + RAW_BUFS - 1 < H:
+                load_head(h + RAW_BUFS - 1)
+            if 1 <= step <= PASSES:
+                quantise_pass(step - 1)
+            if step < PASSES:
+                transpose_pass(step)
+            if not first_of_head and h + 1 < H:
+                prepare_head(h + 1)
+            if step >= MX_LAG:
+                multiply_pass(step - MX_LAG)
+
+        for a in range(ROW_TILES):
+            result = results.tile([P, C], F32, name="result%d" % a, tag="result%d" % a)
+            copy = nc.scalar.copy if a % 2 == 0 else nc.vector.tensor_copy
+            copy(out=result[:], in_=acc[a][:])
+            nc.sync.dma_start(out=out_tiles[a], in_=result[:])

@@ -151,7 +151,7 @@ def tile_fa3mlaattention_pb_k_kernel(tc, x, freqs_cis, w_q, grad_out, out):
                                 ident[:],
                             )
                     last_bank = name == "w" and half == ROW_TILES // 2 - 1
-                    copy = nc.vector.tensor_copy if last_bank and s % PASSES_PER_HEAD == 0 else nc.scalar.copy
+                    copy = nc.vector.tensor_copy if last_bank else nc.scalar.copy
                     copy(
                         out=pairs[:, 2 * half * P : 2 * (half + 1) * P, :],
                         in_=bank[:].rearrange("p u n -> p n u"),

@@ -134,6 +134,8 @@ def tile_fa3mlaattention_pb_k_kernel(tc, x, freqs_cis, w_q, grad_out, out):
             h = s // PASSES_PER_HEAD
             first_word = (s % PASSES_PER_HEAD) * K_PASS // 2
             for name, head_tile in (("g", g_raw[h]), ("w", w_raw[h])):
+                if name == "w":
+                    multiply_next(s, ROW_TILES // 2)
                 words = head_tile[:].bitcast(F32)
                 grouped[name, s] = mx.tile(
                     [P, 4 * TOKENS], BF16, name=name + "_grouped", tag=name + "_grouped", align_bytes=64
@@ -171,18 +173,25 @@ def tile_fa3mlaattention_pb_k_kernel(tc, x, freqs_cis, w_q, grad_out, out):
 
         acc = [sums.tile([P, C], F32, name="acc%d" % a, tag="acc%d" % a) for a in range(ROW_TILES)]
 
-        def multiply_pass(s):
-            for a in range(ROW_TILES):
-                tokens = slice(a * P, (a + 1) * P)
-                nc.tensor.matmul_mx(
-                    out=acc[a][:],
-                    lhsT=codes["g", s][:, tokens].bitcast(E5M2_X4),
-                    lhsT_scale=scales["g", s][:, tokens],
-                    rhs=codes["w", s][:].bitcast(E4M3_X4),
-                    rhs_scale=scales["w", s][:],
-                    start=(s == 0),
-                    stop=(s == PASSES - 1),
-                )
+        def multiply(s, a):
+            tokens = slice(a * P, (a + 1) * P)
+            nc.tensor.matmul_mx(
+                out=acc[a][:],
+                lhsT=codes["g", s][:, tokens].bitcast(E5M2_X4),
+                lhsT_scale=scales["g", s][:, tokens],
+                rhs=codes["w", s][:].bitcast(E4M3_X4),
+                rhs_scale=scales["w", s][:],
+                start=(s == 0),
+                stop=(s == PASSES - 1),
+            )
+
+        waiting = [(s, a) for s in range(PASSES) for a in range(ROW_TILES)]
+
+        def multiply_next(step, count):
+            if step >= MX_LAG:
+                for s, a in waiting[:count]:
+                    multiply(s, a)
+                    waiting.remove((s, a))
 
         prepare_head(0)
         for step in range(PASSES + MX_LAG):
@@ -196,8 +205,7 @@ def tile_fa3mlaattention_pb_k_kernel(tc, x, freqs_cis, w_q, grad_out, out):
                 transpose_pass(step)
             if not first_of_head and h + 1 < H:
                 prepare_head(h + 1)
-            if step >= MX_LAG:
-                multiply_pass(step - MX_LAG)
+            multiply_next(step, ROW_TILES // 2 if step < PASSES else ROW_TILES)
 
         for a in range(ROW_TILES):
             result = results.tile([P, C], F32, name="result%d" % a, tag="result%d" % a)

from contextlib import ExitStack

import concourse.mybir as mybir
from concourse.masks import make_identity

F32 = mybir.dt.float32
BF16 = mybir.dt.bfloat16
U32 = mybir.dt.uint32
U8 = mybir.dt.uint8
E5M2_X4 = mybir.dt.float8_e5m2_x4
E4M3_X4 = mybir.dt.float8_e4m3fn_x4
MULT = mybir.AluOpType.mult
ADD = mybir.AluOpType.add

P = 128
B, T, C, H = 2, 256, 512, 16
DN, DR = 960, 64
DQ = DN + DR
NF = DR // 2
TOKENS = B * T
ROW_TILES = TOKENS // P
T_TILES = T // P

WINDOW = 256
K_PASS = 2 * WINDOW
PASSES = H * DQ // K_PASS
PASSES_PER_HEAD = DQ // K_PASS
BLOCK = 32
RUN = BLOCK // 2
ROT_IN_WINDOW = DN % WINDOW

RAW_BUFS = 8
MX_LAG = 2

FLOPS = 2 * TOKENS * C * H * DQ
BYTES = 2 * (TOKENS + C) * H * DQ + 2 * T * DR + 4 * TOKENS * C


def runs_that_change_places(head_tile):
    words = head_tile[:].bitcast(F32)
    plain = words[:, :, (DN - WINDOW) // 2 : (DN - WINDOW + DR) // 2]
    rotated = words[:, :, DN // 2 : DQ // 2]
    plain_second = plain.rearrange("p a (i c) -> p a i c", c=BLOCK // 2)[:, :, :, RUN // 2 :]
    rotated_first = rotated.rearrange("p a (i c) -> p a i c", c=BLOCK // 2)[:, :, :, : RUN // 2]
    return plain_second, rotated_first


def tile_fa3mlaattention_pb_k_kernel(tc, x, freqs_cis, w_q, grad_out, out):
    nc = tc.nc
    g_heads = grad_out.rearrange("b (t p) h c -> p (b t) h c", p=P)
    w_heads = w_q.rearrange("(a p) (h c) -> p a h c", p=P, c=DQ)
    out_tiles = out.rearrange("b (t p) c -> (b t) p c", p=P)

    with ExitStack() as ctx:
        consts = ctx.enter_context(tc.tile_pool(name="consts", bufs=1))
        raw = ctx.enter_context(tc.tile_pool(name="raw", bufs=RAW_BUFS))
        rot = ctx.enter_context(tc.tile_pool(name="rot", bufs=2))
        mx = ctx.enter_context(tc.tile_pool(name="mx", bufs=MX_LAG + 1))
        results = ctx.enter_context(tc.tile_pool(name="results", bufs=1))
        sums = ctx.enter_context(tc.psum_pool(name="sums", bufs=1))
        flipped = ctx.enter_context(tc.psum_pool(name="flipped", bufs=1))
        ctx.enter_context(tc.manual_schedule())

        g_raw = {}
        w_raw = {}

        def load_head(h):
            g_raw[h] = raw.tile([P, ROW_TILES, DQ], BF16, name="g_raw", tag="g_raw")
            nc.sync.dma_start(out=g_raw[h][:], in_=g_heads[:, :, h, :])
            w_raw[h] = raw.tile([P, ROW_TILES, DQ], BF16, name="w_raw", tag="w_raw")
            nc.sync.dma_start(out=w_raw[h][:], in_=w_heads[:, :, h, :])

        freqs = consts.tile([P, T_TILES, NF, 2], BF16)
        nc.scalar.dma_start(out=freqs[:], in_=freqs_cis.rearrange("(t p) j c -> p t j c", p=P))
        for h in range(RAW_BUFS - 1):
            load_head(h)

        ident = consts.tile([P, P], F32)
        make_identity(nc, ident[:])

        cos_cos = consts.tile([P, T_TILES, 2, NF], BF16)
        nc.vector.tensor_copy(
            out=cos_cos[:], in_=freqs[:, :, :, 0].unsqueeze(2).to_broadcast([P, T_TILES, 2, NF])
        )
        sin_sin = consts.tile([P, T_TILES, 2, NF], BF16)
        nc.vector.tensor_scalar(
            out=sin_sin[:, :, 0, :], in0=freqs[:, :, :, 1], scalar1=-1.0, scalar2=None, op0=MULT
        )
        nc.vector.tensor_copy(out=sin_sin[:, :, 1, :], in_=freqs[:, :, :, 1])

        def for_both_batches(table):
            return (
                table[:]
                .rearrange("p t f j -> p t (f j)")
                .unsqueeze(1)
                .to_broadcast([P, B, T_TILES, DR])
            )

        def prepare_head(h):
            g_tile = g_raw[h]
            g_rot = g_tile[:].rearrange("p (b t) c -> p b t c", b=B)[:, :, :, DN:DQ]
            by_cos = rot.tile([P, B, T_TILES, DR], F32)
            nc.vector.tensor_tensor(out=by_cos[:], in0=g_rot, in1=for_both_batches(cos_cos), op=MULT)
            by_sin = rot.tile([P, B, T_TILES, DR], F32)
            nc.vector.tensor_tensor(out=by_sin[:], in0=g_rot, in1=for_both_batches(sin_sin), op=MULT)

            plain_second, rotated_first = runs_that_change_places(g_tile)
            nc.vector.tensor_copy(out=rotated_first, in_=plain_second)

            split = "p b t (f r m) -> p (b t) f r m"
            cos_runs = by_cos[:].rearrange(split, f=2, r=2)
            sin_runs = by_sin[:].rearrange(split, f=2, r=2)
            windows = g_tile[:, :, K_PASS:DQ].rearrange("p a (r c) -> p a r c", r=2)
            for f in range(2):
                lo = ROT_IN_WINDOW + BLOCK * f + RUN
                nc.vector.tensor_tensor(
                    out=windows[:, :, :, lo : lo + RUN],
                    in0=cos_runs[:, :, f],
                    in1=sin_runs[:, :, 1 - f],
                    op=ADD,
                )

            plain_second, rotated_first = runs_that_change_places(w_raw[h])
            parked = rot.tile([P, ROW_TILES, DR // BLOCK, RUN // 2], F32)
            nc.scalar.copy(out=parked[:], in_=plain_second)
            nc.scalar.copy(out=plain_second, in_=rotated_first)
            nc.scalar.copy(out=rotated_first, in_=parked[:])

        grouped = {}
        codes = {}
        scales = {}

        def transpose_pass(s):
            h = s // PASSES_PER_HEAD
            first_word = (s % PASSES_PER_HEAD) * K_PASS // 2
            for name, head_tile in (("g", g_raw[h]), ("w", w_raw[h])):
                if name == "w":
                    multiply_next(s, ROW_TILES // 2)
                words = head_tile[:].bitcast(F32)
                grouped[name, s] = mx.tile(
                    [P, 4 * TOKENS], BF16, name=name + "_grouped", tag=name + "_grouped", align_bytes=64
                )
                pairs = grouped[name, s][:].bitcast(F32).rearrange("p (n u) -> p n u", u=2)
                for half in range(ROW_TILES // 2):
                    bank_name = "%s_bank%d" % (name, half)
                    bank = flipped.tile([P, 2, 2 * P], F32, name=bank_name, tag=bank_name)
                    for i in range(2):
                        for u in range(2):
                            lo = first_word + u * P
                            nc.tensor.transpose(
                                bank[:, u, i * P : (i + 1) * P],
                                words[:, 2 * half + i, lo : lo + P],
                                ident[:],
                            )
                    last_bank = name == "w" and half == ROW_TILES // 2 - 1
                    copy = nc.vector.tensor_copy if last_bank else nc.scalar.copy
                    copy(
                        out=pairs[:, 2 * half * P : 2 * (half + 1) * P, :],
                        in_=bank[:].rearrange("p u n -> p n u"),
                    )

        def quantise_pass(s):
            for name, fp8 in (("g", E5M2_X4), ("w", E4M3_X4)):
                codes[name, s] = mx.tile(
                    [P, TOKENS], U32, name=name + "_codes", tag=name + "_codes", align_bytes=64
                )
                scales[name, s] = mx.tile(
                    [P, TOKENS], U8, name=name + "_scales", tag=name + "_scales", align_bytes=64
                )
                nc.vector.quantize_mx(
                    out=codes[name, s][:].bitcast(fp8), scales=scales[name, s][:], in_=grouped[name, s][:]
                )

        acc = [sums.tile([P, C], F32, name="acc%d" % a, tag="acc%d" % a) for a in range(ROW_TILES)]

        def multiply(s, a):
            tokens = slice(a * P, (a + 1) * P)
            nc.tensor.matmul_mx(
                out=acc[a][:],
                lhsT=codes["g", s][:, tokens].bitcast(E5M2_X4),
                lhsT_scale=scales["g", s][:, tokens],
                rhs=codes["w", s][:].bitcast(E4M3_X4),
                rhs_scale=scales["w", s][:],
                start=(s == 0),
                stop=(s == PASSES - 1),
            )

        waiting = [(s, a) for s in range(PASSES) for a in range(ROW_TILES)]

        def multiply_next(step, count):
            if step >= MX_LAG:
                for s, a in waiting[:count]:
                    multiply(s, a)
                    waiting.remove((s, a))

        prepare_head(0)
        for step in range(PASSES + MX_LAG):
            h = step // PASSES_PER_HEAD
            first_of_head = step % PASSES_PER_HEAD == 0
            if first_of_head and h + RAW_BUFS - 1 < H:
                load_head(h + RAW_BUFS - 1)
            if 1 <= step <= PASSES:
                quantise_pass(step - 1)
            if step < PASSES:
                transpose_pass(step)
            if not first_of_head and h + 1 < H:
                prepare_head(h + 1)
            multiply_next(step, ROW_TILES // 2 if step < PASSES else ROW_TILES)

        for a in range(ROW_TILES):
            result = results.tile([P, C], F32, name="result%d" % a, tag="result%d" % a)
            copy = nc.scalar.copy if a % 2 == 0 else nc.vector.tensor_copy
            copy(out=result[:], in_=acc[a][:])
            nc.sync.dma_start(out=out_tiles[a], in_=result[:])
